import numpy as np
import ml_dtypes


def mxq(x, axis, fmt="e4m3"):
    dtype, down = {"e4m3": (ml_dtypes.float8_e4m3fn, 7), "e5m2": (ml_dtypes.float8_e5m2, 14)}[fmt]
    v = np.moveaxis(np.asarray(x, np.float32).astype(ml_dtypes.bfloat16).astype(np.float64), axis, -1)
    blocks = v.reshape(v.shape[:-1] + (-1, 32))
    amax = np.abs(blocks).max(-1, keepdims=True)
    byte = np.maximum(np.where(amax > 0, np.frexp(amax)[1] - 1 + 127, 0) - down, 1)
    scale = np.exp2(byte - 127.0)
    codes = (blocks / scale).astype(np.float32).astype(dtype).astype(np.float64)
    return np.moveaxis((codes * scale).reshape(v.shape), -1, axis)


WIDE = False


def mx_kscale(k):
    if not WIDE:
        return np.ones(k)
    levels = np.array([10, -10, 5, -5, 0])
    a = np.random.permutation(np.resize(levels, k // 512 * 4)).reshape(k // 512, 4)
    idx = np.arange(k)
    return np.exp2(a[idx // 512, idx % 128 // 32])


BF16 = ml_dtypes.bfloat16


def bf(x):
    return np.asarray(x, np.float32).astype(BF16)


def f64(x):
    return np.asarray(x).astype(np.float64)


G, D1, D2, D3, K, N = 16, 2, 8, 8, 512, 512

EPS = 1e-6


def setup_inputs():
    s = mx_kscale(K)
    rows = np.random.standard_normal((G, D1, D2, D3, K))
    rows = rows * (0.5 + 1.5 * np.random.random_sample((G, D1, D2, D3, 1))) + 0.5 * np.random.standard_normal((G, D1, D2, D3, 1))
    return {"x": bf(rows.reshape(G * K, D1, D2, D3)),
            "ln_gamma": bf((1.0 + 0.1 * np.random.standard_normal((G, K))) * s),
            "ln_beta": bf(0.1 * np.random.standard_normal((G, K)) * s),
            "W": bf(np.random.standard_normal((G, N, K)) / np.sqrt(K) / s),
            "b": bf(0.1 * np.random.standard_normal((G, N)))}


def reference(x, ln_gamma, ln_beta, W, b):
    xg = f64(x).reshape(G, D1, D2, D3, K)
    mu = np.mean(xg, axis=-1, keepdims=True)
    var = np.mean(np.square(xg - mu), axis=-1, keepdims=True)
    xn = (xg - mu) / np.sqrt(var + EPS)
    xn = xn * f64(ln_gamma)[:, None, None, None, :] + f64(ln_beta)[:, None, None, None, :]
    a = mxq(xn.reshape(G, D1 * D2 * D3, K), 2, "e4m3")
    y = a @ mxq(f64(W), 2, "e4m3").transpose(0, 2, 1)
    y = y.reshape(G, D1, D2, D3, N) + f64(b)[:, None, None, None, :]
    y = np.moveaxis(y, 0, -2).reshape(D1, D2, D3, G * N)
    return np.transpose(y, (3, 0, 1, 2))

@@ -1,0 +1,210 @@
+from contextlib import ExitStack
+
+import concourse.mybir as mybir
+from concourse.masks import make_identity
+
+F32 = mybir.dt.float32
+BF16 = mybir.dt.bfloat16
+U32 = mybir.dt.uint32
+U8 = mybir.dt.uint8
+FP8X4 = mybir.dt.float8_e4m3fn_x4
+ALU = mybir.AluOpType
+ACT = mybir.ActivationFunctionType
+
+G = 16
+P = 128
+K = 512
+N = 512
+EPS = 1e-6
+FLOPS = 2 * G * P * K * N
+
+XB = 4
+OUT_ON_SCALAR = (3, 7, 11, 15)
+W_ON_VECTOR = ()
+
+
+def tile_groupedlinear_kernel(tc, x, ln_gamma, ln_beta, W, b, out):
+    nc = tc.nc
+    x_v = x.rearrange("(g p j) b c d -> p g (j b c d)", g=G, p=P, j=4)
+    w_v = W.rearrange("g (p t) k -> p g (t k)", t=4)
+    o_v = out.rearrange("(g p t) b c d -> p g (t b c d)", g=G, p=P, t=4)
+
+    with ExitStack() as es:
+        const = es.enter_context(tc.tile_pool(name="const", bufs=1))
+        xin = es.enter_context(tc.tile_pool(name="xin", bufs=1))
+        win = es.enter_context(tc.tile_pool(name="win", bufs=1))
+        xwork = es.enter_context(tc.tile_pool(name="xwork", bufs=2))
+        xkeep = es.enter_context(tc.tile_pool(name="xkeep", bufs=1))
+        wwork = es.enter_context(tc.tile_pool(name="wwork", bufs=4))
+        owork = es.enter_context(tc.tile_pool(name="owork", bufs=6))
+        ps_w = es.enter_context(tc.psum_pool(name="ps_w", bufs=4))
+        ps_x = es.enter_context(tc.psum_pool(name="ps_x", bufs=2))
+        ps_o = es.enter_context(tc.psum_pool(name="ps_o", bufs=2))
+
+        eps_t = const.tile([P, 1], F32, name="eps_t")
+        nc.vector.memset(eps_t[:], EPS)
+        warm = const.tile([P, 1], F32, name="warm")
+        nc.scalar.activation(out=warm[:], in_=eps_t[:], func=ACT.Sqrt)
+        prm = const.tile([P, K], BF16, name="prm")
+        nc.vector.memset(prm[:], 0.0)
+        ident = const.tile([P, P], F32, name="ident")
+        make_identity(nc, ident[:])
+
+        nc.scalar.dma_start(out=prm[0:G, :], in_=ln_gamma)
+        nc.scalar.dma_start(out=prm[G:2 * G, :], in_=ln_beta)
+        nc.scalar.dma_start(out=prm[2 * G:3 * G, :], in_=b)
+
+        xbs = []
+        wraw = []
+
+        def load_x(bi):
+            t = xin.tile([P, XB, K], BF16, name="xb%d" % bi)
+            nc.sync.dma_start(out=t[:], in_=x_v[:, XB * bi:XB * (bi + 1), :])
+            xbs.append(t)
+
+        def load_w(g):
+            t = win.tile([P, 4 * K], BF16, name="wr%d" % g)
+            nc.sync.dma_start(out=t[:], in_=w_v[:, g, :])
+            wraw.append(t)
+
+        load_x(0)
+        load_w(0)
+        load_w(1)
+        load_x(1)
+        load_w(2)
+        load_w(3)
+        load_x(2)
+        load_w(4)
+        load_w(5)
+        load_x(3)
+        for g in range(6, G):
+            load_w(g)
+
+        prm_w = prm[:].bitcast(F32)
+        p_t = ps_x.tile([P, 4, P], F32, name="xT")
+        nc.tensor.transpose(p_t[:, 0, :], prm_w[:, 0:P], ident[:])
+        nc.tensor.transpose(p_t[:, 1, :], prm_w[:, P:2 * P], ident[:])
+        nc.tensor.transpose(p_t[:, 2, :], prm_w[:, 0:2 * P:2], ident[:])
+        nc.tensor.transpose(p_t[:, 3, :], prm_w[:, 1:2 * P:2], ident[:])
+        p_b = p_t[:].rearrange("q j r -> q (j r)").bitcast(BF16).rearrange("q (j r e) -> q j r e", j=4, e=2)
+        gb_t = const.tile([P, 2 * G, 4], F32, name="gb_t")
+        bias_t = const.tile([P, G, 4], F32, name="bias_t")
+        nc.vector.tensor_copy(
+            out=gb_t[:].rearrange("q r (u e) -> q r u e", u=2),
+            in_=p_b[:, 0:2, 0:2 * G, :].rearrange("q u r e -> q r u e"),
+        )
+        nc.vector.tensor_copy(
+            out=bias_t[:].rearrange("q r (u e) -> q r u e", u=2),
+            in_=p_b[:, 2:4, 2 * G:3 * G, :].rearrange("q u r e -> q r u e"),
+        )
+
+        stats = const.tile([P, G, 6], F32, name="stats")
+        mv = const.tile([P, G, 2], F32, name="mv")
+        std = const.tile([P, G, 1], F32, name="std")
+        rstd = const.tile([P, G, 1], F32, name="rstd")
+        negmu = const.tile([P, G, 1], F32, name="negmu")
+
+        xcs = []
+        xss = []
+
+        def x_path(bi):
+            xb = xbs[bi]
+            for i in range(XB):
+                nc.vector.bn_stats(out=stats[:, XB * bi + i, :], in_=xb[:, i, :])
+            for i in range(XB):
+                g = XB * bi + i
+                nc.vector.bn_aggr(out=mv[:, g, :], in_=stats[:, g, :])
+            sl = slice(XB * bi, XB * (bi + 1))
+            nc.scalar.activation(out=std[:, sl, :], in_=mv[:, sl, 1:2], func=ACT.Sqrt, bias=eps_t[:, 0:1], scale=1.0)
+            nc.vector.reciprocal(out=rstd[:, sl, :], in_=std[:, sl, :])
+            nc.vector.tensor_scalar(out=negmu[:, sl, :], in0=mv[:, sl, 0:1], scalar1=-1.0, scalar2=None, op0=ALU.mult)
+            xp = xwork.tile([P, XB, 4, P], BF16, name="xp")
+            for i in range(XB):
+                g = XB * bi + i
+                xh = xwork.tile([P, K], F32, name="xh", bufs=4)
+                nc.gpsimd.tensor_scalar(
+                    out=xh[:].rearrange("p (u e q) -> p u e q", u=2, e=2),
+                    in0=xb[:, i, :].rearrange("p (u q e) -> p u e q", u=2, e=2),
+                    scalar1=negmu[:, g, :],
+                    scalar2=rstd[:, g, :],
+                    op0=ALU.add,
+                    op1=ALU.mult,
+                )
+                x_t = ps_x.tile([P, 4, P], F32, name="xT")
+                for t in range(4):
+                    nc.tensor.transpose(x_t[:, t, :], xh[:, t * P:(t + 1) * P], ident[:])
+                for t in range(4):
+                    nc.scalar.activation(
+                        out=xp[:, i, t, :],
+                        in_=x_t[:, t, :],
+                        func=ACT.Identity,
+                        scale=gb_t[:, g, t:t + 1],
+                        bias=gb_t[:, G + g, t:t + 1],
+                    )
+            xg = xwork.tile([P, XB, P, 4], BF16, name="xg", align_bytes=64)
+            nc.vector.tensor_copy(out=xg[:], in_=xp[:].rearrange("p g t r -> p g r t"))
+            xc = xkeep.tile([P, XB * P], U32, name="xc%d" % bi, align_bytes=64)
+            xs = xkeep.tile([P, XB * P], U8, name="xs%d" % bi, align_bytes=64)
+            nc.vector.quantize_mx(
+                out=xc[:].bitcast(FP8X4), scales=xs[:], in_=xg[:].rearrange("p g r t -> p (g r t)")
+            )
+            xcs.append(xc)
+            xss.append(xs)
+
+        wcs = {}
+
+        def w_path(g):
+            wf = wraw[g][:].bitcast(F32)
+            wg = wwork.tile([P, 4 * N], BF16, name="wg", align_bytes=64)
+            wgf = wg[:].bitcast(F32)
+            for h in range(2):
+                w_t = ps_w.tile([P, 2, 2, P], F32, name="wT")
+                for tt in range(2):
+                    for u in range(2):
+                        c0 = (2 * h + tt) * 256 + u * P
+                        nc.tensor.transpose(w_t[:, tt, u, :], wf[:, c0:c0 + P], ident[:])
+                dst = wgf[:, h * 512:(h + 1) * 512].rearrange("q (tt p u) -> q tt p u", tt=2, u=2)
+                src = w_t[:].rearrange("q tt u p -> q tt p u")
+                if (g, h) in W_ON_VECTOR:
+                    nc.vector.tensor_copy(out=dst, in_=src)
+                else:
+                    nc.scalar.copy(out=dst, in_=src)
+            wc = wwork.tile([P, N], U32, name="wc", align_bytes=64)
+            ws = wwork.tile([P, N], U8, name="ws", align_bytes=64)
+            nc.vector.quantize_mx(out=wc[:].bitcast(FP8X4), scales=ws[:], in_=wg[:])
+            wcs[g] = (wc, ws)
+
+        def mx(g):
+            wc, ws = wcs[g]
+            xc = xcs[g // XB]
+            xs = xss[g // XB]
+            i = g % XB
+            acc = ps_o.tile([P, 4, P], F32, name="acc")
+            for t in range(4):
+                nc.tensor.matmul_mx(
+                    out=acc[:, t, :],
+                    lhsT=wc[:, t * P:(t + 1) * P].bitcast(FP8X4),
+                    lhsT_scale=ws[:, t * P:(t + 1) * P],
+                    rhs=xc[:, i * P:(i + 1) * P].bitcast(FP8X4),
+                    rhs_scale=xs[:, i * P:(i + 1) * P],
+                    start=True,
+                    stop=True,
+                )
+            ot = owork.tile([P, 4, P], F32, name="ot")
+            if g in OUT_ON_SCALAR:
+                for t in range(4):
+                    nc.scalar.activation(
+                        out=ot[:, t, :], in_=acc[:, t, :], func=ACT.Identity, bias=bias_t[:, g, t:t + 1], scale=1.0
+                    )
+            else:
+                nc.vector.tensor_tensor(
+                    out=ot[:], in0=acc[:], in1=bias_t[:, g, :].unsqueeze(2).to_broadcast([P, 4, P]), op=ALU.add
+                )
+            nc.sync.dma_start(out=o_v[:, g, :], in_=ot[:].rearrange("p t r -> p (t r)"))
+
+        x_path(0)
+        for g in range(G):
+            w_path(g)
+            if g in (1, 3, 5):
+                x_path((g + 1) // 2)
+            mx(g)

@@ -19,8 +19,22 @@ EPS = 1e-6
 FLOPS = 2 * G * P * K * N
 
 XB = 4
+NB = G // XB
 OUT_ON_SCALAR = (3, 7, 11, 15)
-W_ON_VECTOR = ()
+DUMMY = 1
+L_BS = 12
+L_SQ = 11
+L_RC = 11
+L_XH = 7
+L_XT = 6
+L_XE = 5
+L_RG = 4
+L_XQ = 4
+L_WT = 4
+L_WE = 3
+L_WQ = 2
+H0 = 3
+HS = 3
 
 
 def tile_groupedlinear_kernel(tc, x, ln_gamma, ln_beta, W, b, out):
@@ -34,152 +48,196 @@ def tile_groupedlinear_kernel(tc, x, ln_gamma, ln_beta, W, b, out):
         xin = es.enter_context(tc.tile_pool(name="xin", bufs=1))
         win = es.enter_context(tc.tile_pool(name="win", bufs=1))
         xwork = es.enter_context(tc.tile_pool(name="xwork", bufs=2))
-        xkeep = es.enter_context(tc.tile_pool(name="xkeep", bufs=1))
-        wwork = es.enter_context(tc.tile_pool(name="wwork", bufs=4))
+        keep = es.enter_context(tc.tile_pool(name="keep", bufs=1))
+        wwork = es.enter_context(tc.tile_pool(name="wwork", bufs=6))
         owork = es.enter_context(tc.tile_pool(name="owork", bufs=6))
         ps_w = es.enter_context(tc.psum_pool(name="ps_w", bufs=4))
         ps_x = es.enter_context(tc.psum_pool(name="ps_x", bufs=2))
         ps_o = es.enter_context(tc.psum_pool(name="ps_o", bufs=2))
+        es.enter_context(tc.manual_schedule())
+
+        prm = const.tile([P, K], BF16, name="prm")
+        nc.scalar.dma_start(out=prm[0:G, :], in_=ln_gamma)
+        nc.scalar.dma_start(out=prm[G:2 * G, :], in_=ln_beta)
+        nc.scalar.dma_start(out=prm[2 * G:3 * G, :], in_=b)
+        nc.scalar.dma_start(out=prm[3 * G:4 * G, :], in_=b)
+
+        xbs = []
+        wraw = []
+        for bi in range(NB):
+            xbs.append(xin.tile([P, XB, K], BF16, name="xb%d" % bi))
+        for g in range(G):
+            wraw.append(win.tile([P, 4 * K], BF16, name="wr%d" % g))
+
+        def load_x(bi, lo, hi):
+            nc.sync.dma_start(out=xbs[bi][:, lo:hi, :], in_=x_v[:, XB * bi + lo:XB * bi + hi, :])
+
+        def load_w(g, lo, hi):
+            nc.sync.dma_start(out=wraw[g][:, lo:hi], in_=w_v[:, g, lo:hi])
+
+        load_x(0, 0, 2)
+        load_x(0, 2, 4)
+        load_w(0, 0, 2 * K)
+        load_w(0, 2 * K, 4 * K)
+        for bi in range(1, NB):
+            load_x(bi, 0, XB)
+            load_w(bi, 0, 4 * K)
+        for g in range(NB, G):
+            load_w(g, 0, 4 * K)
 
         eps_t = const.tile([P, 1], F32, name="eps_t")
         nc.vector.memset(eps_t[:], EPS)
         warm = const.tile([P, 1], F32, name="warm")
         nc.scalar.activation(out=warm[:], in_=eps_t[:], func=ACT.Sqrt)
-        prm = const.tile([P, K], BF16, name="prm")
-        nc.vector.memset(prm[:], 0.0)
+        nc.vector.memset(prm[4 * G:P, :], 0.0)
+        if DUMMY:
+            zb = const.tile([P, 4 * N], BF16, name="zb", align_bytes=64)
+            zc = const.tile([P, N], U32, name="zc", align_bytes=64)
+            zs = const.tile([P, N], U8, name="zs", align_bytes=64)
+            nc.vector.memset(zb[:], 0.0)
+            nc.vector.quantize_mx(out=zc[:].bitcast(FP8X4), scales=zs[:], in_=zb[:])
         ident = const.tile([P, P], F32, name="ident")
         make_identity(nc, ident[:])
 
-        nc.scalar.dma_start(out=prm[0:G, :], in_=ln_gamma)
-        nc.scalar.dma_start(out=prm[G:2 * G, :], in_=ln_beta)
-        nc.scalar.dma_start(out=prm[2 * G:3 * G, :], in_=b)
-
-        xbs = []
-        wraw = []
-
-        def load_x(bi):
-            t = xin.tile([P, XB, K], BF16, name="xb%d" % bi)
-            nc.sync.dma_start(out=t[:], in_=x_v[:, XB * bi:XB * (bi + 1), :])
-            xbs.append(t)
-
-        def load_w(g):
-            t = win.tile([P, 4 * K], BF16, name="wr%d" % g)
-            nc.sync.dma_start(out=t[:], in_=w_v[:, g, :])
-            wraw.append(t)
-
-        load_x(0)
-        load_w(0)
-        load_w(1)
-        load_x(1)
-        load_w(2)
-        load_w(3)
-        load_x(2)
-        load_w(4)
-        load_w(5)
-        load_x(3)
-        for g in range(6, G):
-            load_w(g)
-
-        prm_w = prm[:].bitcast(F32)
-        p_t = ps_x.tile([P, 4, P], F32, name="xT")
-        nc.tensor.transpose(p_t[:, 0, :], prm_w[:, 0:P], ident[:])
-        nc.tensor.transpose(p_t[:, 1, :], prm_w[:, P:2 * P], ident[:])
-        nc.tensor.transpose(p_t[:, 2, :], prm_w[:, 0:2 * P:2], ident[:])
-        nc.tensor.transpose(p_t[:, 3, :], prm_w[:, 1:2 * P:2], ident[:])
-        p_b = p_t[:].rearrange("q j r -> q (j r)").bitcast(BF16).rearrange("q (j r e) -> q j r e", j=4, e=2)
         gb_t = const.tile([P, 2 * G, 4], F32, name="gb_t")
         bias_t = const.tile([P, G, 4], F32, name="bias_t")
-        nc.vector.tensor_copy(
-            out=gb_t[:].rearrange("q r (u e) -> q r u e", u=2),
-            in_=p_b[:, 0:2, 0:2 * G, :].rearrange("q u r e -> q r u e"),
-        )
-        nc.vector.tensor_copy(
-            out=bias_t[:].rearrange("q r (u e) -> q r u e", u=2),
-            in_=p_b[:, 2:4, 2 * G:3 * G, :].rearrange("q u r e -> q r u e"),
-        )
-
         stats = const.tile([P, G, 6], F32, name="stats")
         mv = const.tile([P, G, 2], F32, name="mv")
         std = const.tile([P, G, 1], F32, name="std")
         rstd = const.tile([P, G, 1], F32, name="rstd")
         negmu = const.tile([P, G, 1], F32, name="negmu")
 
-        xcs = []
-        xss = []
+        def params_pe():
+            prm_w = prm[:].bitcast(F32)
+            p_t = ps_x.tile([P, 4, P], F32, name="xT")
+            nc.tensor.transpose(p_t[:, 0, :], prm_w[:, 0:P], ident[:])
+            nc.tensor.transpose(p_t[:, 1, :], prm_w[:, P:2 * P], ident[:])
+            nc.tensor.transpose(p_t[:, 2, :], prm_w[:, 0:2 * P:2], ident[:])
+            nc.tensor.transpose(p_t[:, 3, :], prm_w[:, 1:2 * P:2], ident[:])
+            return p_t
 
-        def x_path(bi):
-            xb = xbs[bi]
-            for i in range(XB):
-                nc.vector.bn_stats(out=stats[:, XB * bi + i, :], in_=xb[:, i, :])
-            for i in range(XB):
-                g = XB * bi + i
-                nc.vector.bn_aggr(out=mv[:, g, :], in_=stats[:, g, :])
+        def params_out(p_t):
+            p_b = p_t[:].rearrange("q j r -> q (j r)").bitcast(BF16).rearrange("q (j r e) -> q j r e", j=4, e=2)
+            nc.vector.tensor_copy(
+                out=gb_t[:].rearrange("q r (u e) -> q r u e", u=2),
+                in_=p_b[:, 0:2, 0:2 * G, :].rearrange("q u r e -> q r u e"),
+            )
+            nc.vector.tensor_copy(
+                out=bias_t[:].rearrange("q r (u e) -> q r u e", u=2),
+                in_=p_b[:, 2:4, 2 * G:3 * G, :].rearrange("q u r e -> q r u e"),
+            )
+
+        xh_t = {}
+        xt_t = {}
+        xp_t = {}
+        xg_t = {}
+        xc_t = {}
+        wt_t = {}
+        wg_t = {}
+        wc_t = {}
+        acc_t = {}
+
+        def st_bs(j):
+            nc.vector.bn_stats(out=stats[:, j, :], in_=xbs[j // XB][:, j % XB, :])
+            nc.vector.bn_aggr(out=mv[:, j, :], in_=stats[:, j, :])
+
+        def st_sq(bi):
             sl = slice(XB * bi, XB * (bi + 1))
             nc.scalar.activation(out=std[:, sl, :], in_=mv[:, sl, 1:2], func=ACT.Sqrt, bias=eps_t[:, 0:1], scale=1.0)
+
+        def st_rc(bi):
+            sl = slice(XB * bi, XB * (bi + 1))
             nc.vector.reciprocal(out=rstd[:, sl, :], in_=std[:, sl, :])
             nc.vector.tensor_scalar(out=negmu[:, sl, :], in0=mv[:, sl, 0:1], scalar1=-1.0, scalar2=None, op0=ALU.mult)
-            xp = xwork.tile([P, XB, 4, P], BF16, name="xp")
-            for i in range(XB):
-                g = XB * bi + i
-                xh = xwork.tile([P, K], F32, name="xh", bufs=4)
-                nc.gpsimd.tensor_scalar(
-                    out=xh[:].rearrange("p (u e q) -> p u e q", u=2, e=2),
-                    in0=xb[:, i, :].rearrange("p (u q e) -> p u e q", u=2, e=2),
-                    scalar1=negmu[:, g, :],
-                    scalar2=rstd[:, g, :],
-                    op0=ALU.add,
-                    op1=ALU.mult,
-                )
-                x_t = ps_x.tile([P, 4, P], F32, name="xT")
-                for t in range(4):
-                    nc.tensor.transpose(x_t[:, t, :], xh[:, t * P:(t + 1) * P], ident[:])
-                for t in range(4):
-                    nc.scalar.activation(
-                        out=xp[:, i, t, :],
-                        in_=x_t[:, t, :],
-                        func=ACT.Identity,
-                        scale=gb_t[:, g, t:t + 1],
-                        bias=gb_t[:, G + g, t:t + 1],
-                    )
-            xg = xwork.tile([P, XB, P, 4], BF16, name="xg", align_bytes=64)
-            nc.vector.tensor_copy(out=xg[:], in_=xp[:].rearrange("p g t r -> p g r t"))
-            xc = xkeep.tile([P, XB * P], U32, name="xc%d" % bi, align_bytes=64)
-            xs = xkeep.tile([P, XB * P], U8, name="xs%d" % bi, align_bytes=64)
-            nc.vector.quantize_mx(
-                out=xc[:].bitcast(FP8X4), scales=xs[:], in_=xg[:].rearrange("p g r t -> p (g r t)")
+
+        def st_xh(j):
+            xh = xwork.tile([P, K], F32, name="xh", bufs=4)
+            nc.gpsimd.tensor_scalar(
+                out=xh[:].rearrange("p (u e q) -> p u e q", u=2, e=2),
+                in0=xbs[j // XB][:, j % XB, :].rearrange("p (u q e) -> p u e q", u=2, e=2),
+                scalar1=negmu[:, j, :],
+                scalar2=rstd[:, j, :],
+                op0=ALU.add,
+                op1=ALU.mult,
             )
-            xcs.append(xc)
-            xss.append(xs)
+            xh_t[j] = xh
 
-        wcs = {}
+        def st_xt(j):
+            x_t = ps_x.tile([P, 4, P], F32, name="xT")
+            for t in range(4):
+                nc.tensor.transpose(x_t[:, t, :], xh_t[j][:, t * P:(t + 1) * P], ident[:])
+            xt_t[j] = x_t
 
-        def w_path(g):
+        def st_xe(j):
+            bi = j // XB
+            if j % XB == 0:
+                xp_t[bi] = xwork.tile([P, 4, XB, P], BF16, name="xp")
+            for t in range(4):
+                nc.scalar.activation(
+                    out=xp_t[bi][:, t, j % XB, :],
+                    in_=xt_t[j][:, t, :],
+                    func=ACT.Identity,
+                    scale=gb_t[:, j, t:t + 1],
+                    bias=gb_t[:, G + j, t:t + 1],
+                )
+
+        def st_rg(bi):
+            xg = xwork.tile([P, XB * P * 4], BF16, name="xg", align_bytes=64)
+            nc.vector.tensor_copy(
+                out=xg[:].rearrange("p (c i t) -> p c t i", i=4, t=4),
+                in_=xp_t[bi][:].rearrange("p t g r -> p t (g r)").rearrange("p t (c i) -> p c t i", i=4),
+            )
+            xg_t[bi] = xg
+
+        def st_xq(bi):
+            xc = keep.tile([P, XB * P], U32, name="xc%d" % bi, align_bytes=64)
+            xs = keep.tile([P, XB * P], U8, name="xs%d" % bi, align_bytes=64)
+            nc.vector.quantize_mx(out=xc[:].bitcast(FP8X4), scales=xs[:], in_=xg_t[bi][:])
+            xc_t[bi] = (xc, xs)
+
+        def st_wt(g):
             wf = wraw[g][:].bitcast(F32)
-            wg = wwork.tile([P, 4 * N], BF16, name="wg", align_bytes=64)
-            wgf = wg[:].bitcast(F32)
             for h in range(2):
                 w_t = ps_w.tile([P, 2, 2, P], F32, name="wT")
                 for tt in range(2):
                     for u in range(2):
                         c0 = (2 * h + tt) * 256 + u * P
                         nc.tensor.transpose(w_t[:, tt, u, :], wf[:, c0:c0 + P], ident[:])
-                dst = wgf[:, h * 512:(h + 1) * 512].rearrange("q (tt p u) -> q tt p u", tt=2, u=2)
-                src = w_t[:].rearrange("q tt u p -> q tt p u")
-                if (g, h) in W_ON_VECTOR:
-                    nc.vector.tensor_copy(out=dst, in_=src)
-                else:
-                    nc.scalar.copy(out=dst, in_=src)
-            wc = wwork.tile([P, N], U32, name="wc", align_bytes=64)
-            ws = wwork.tile([P, N], U8, name="ws", align_bytes=64)
-            nc.vector.quantize_mx(out=wc[:].bitcast(FP8X4), scales=ws[:], in_=wg[:])
-            wcs[g] = (wc, ws)
+                wt_t[(g, h)] = w_t
 
-        def mx(g):
-            wc, ws = wcs[g]
-            xc = xcs[g // XB]
-            xs = xss[g // XB]
-            i = g % XB
+        def st_we(g):
+            wg = wwork.tile([P, 4 * N], BF16, name="wg", align_bytes=64)
+            wgf = wg[:].bitcast(F32)
+            for h in range(2):
+                nc.scalar.copy(
+                    out=wgf[:, h * 512:(h + 1) * 512].rearrange("q (tt p u) -> q tt p u", tt=2, u=2),
+                    in_=wt_t[(g, h)][:].rearrange("q tt u p -> q tt p u"),
+                )
+            wg_t[g] = wg
+
+        def st_wq(g):
+            wc = keep.tile([P, N], U32, name="wc%d" % g, align_bytes=64)
+            ws = keep.tile([P, N], U8, name="ws%d" % g, align_bytes=64)
+            nc.vector.quantize_mx(out=wc[:].bitcast(FP8X4), scales=ws[:], in_=wg_t[g][:])
+            wc_t[g] = (wc, ws)
+
+        def st_mx(g):
             acc = ps_o.tile([P, 4, P], F32, name="acc")
+            for d in range(DUMMY):
+                nc.tensor.matmul_mx(
+                    out=acc[:].rearrange("p t r -> p (t r)"),
+                    lhsT=zc[:, 0:P].bitcast(FP8X4),
+                    lhsT_scale=zs[:, 0:P],
+                    rhs=zc[:].bitcast(FP8X4),
+                    rhs_scale=zs[:],
+                    start=True,
+                    stop=True,
+                )
+            if g < 0:
+                return
+            wc, ws = wc_t[g]
+            xc, xs = xc_t[g // XB]
+            i = g % XB
             for t in range(4):
                 nc.tensor.matmul_mx(
                     out=acc[:, t, :],
@@ -190,6 +248,10 @@ def tile_groupedlinear_kernel(tc, x, ln_gamma, ln_beta, W, b, out):
                     start=True,
                     stop=True,
                 )
+            acc_t[g] = acc
+
+        def st_oe(g):
+            acc = acc_t[g]
             ot = owork.tile([P, 4, P], F32, name="ot")
             if g in OUT_ON_SCALAR:
                 for t in range(4):
@@ -202,9 +264,57 @@ def tile_groupedlinear_kernel(tc, x, ln_gamma, ln_beta, W, b, out):
                 )
             nc.sync.dma_start(out=o_v[:, g, :], in_=ot[:].rearrange("p t r -> p (t r)"))
 
-        x_path(0)
-        for g in range(G):
-            w_path(g)
-            if g in (1, 3, 5):
-                x_path((g + 1) // 2)
-            mx(g)
+        def group_at(s, lead):
+            j = s + lead
+            return j if 0 <= j < G else None
+
+        def batch_at(s, lead):
+            j = s + lead
+            return j // XB if (0 <= j < G and j % XB == XB - 1) else None
+
+        def w_groups_at(s, lead):
+            return [g for g in range(G) if min(g - lead, H0 - L_BS + HS * g) == s]
+
+        first = -L_BS
+        for s in range(first, G):
+            for g in w_groups_at(s, L_WT):
+                st_wt(g)
+            if s == first + H0 + 1:
+                p_t = params_pe()
+            j = group_at(s, L_XT)
+            if j is not None:
+                st_xt(j)
+            if s >= 0 or DUMMY:
+                st_mx(s)
+            for g in w_groups_at(s, L_WE):
+                st_we(g)
+            bi = batch_at(s, L_SQ)
+            if bi is not None:
+                st_sq(bi)
+            j = group_at(s, L_XE)
+            if j is not None:
+                st_xe(j)
+            if s >= 0 and s in OUT_ON_SCALAR:
+                st_oe(s)
+            j = group_at(s, L_BS)
+            if j is not None:
+                st_bs(j)
+            if s == first + H0 + 1:
+                params_out(p_t)
+            bi = batch_at(s, L_RC)
+            if bi is not None:
+                st_rc(bi)
+            j = group_at(s, L_XH)
+            if j is not None:
+                st_xh(j)
+            j = group_at(s, L_WQ)
+            if j is not None:
+                st_wq(j)
+            bi = batch_at(s, L_RG)
+            if bi is not None:
+                st_rg(bi)
+            if s >= 0 and s not in OUT_ON_SCALAR:
+                st_oe(s)
+            bi = batch_at(s, L_XQ)
+            if bi is not None:
+                st_xq(bi)

@@ -22,6 +22,7 @@ XB = 4
 NB = G // XB
 OUT_ON_SCALAR = (3, 7, 11, 15)
 DUMMY = 1
+DUMMY_HEAD = 2
 L_BS = 12
 L_SQ = 11
 L_RC = 11
@@ -223,7 +224,7 @@ def tile_groupedlinear_kernel(tc, x, ln_gamma, ln_beta, W, b, out):
 
         def st_mx(g):
             acc = ps_o.tile([P, 4, P], F32, name="acc")
-            for d in range(DUMMY):
+            for d in range(DUMMY if g >= 0 else DUMMY_HEAD):
                 nc.tensor.matmul_mx(
                     out=acc[:].rearrange("p t r -> p (t r)"),
                     lhsT=zc[:, 0:P].bitcast(FP8X4),

@@ -21,8 +21,7 @@ FLOPS = 2 * G * P * K * N
 XB = 4
 NB = G // XB
 OUT_ON_SCALAR = (3, 7, 11, 15)
-DUMMY = 1
-DUMMY_HEAD = 2
+DUMMY = 0
 L_BS = 12
 L_SQ = 11
 L_RC = 11
@@ -224,7 +223,7 @@ def tile_groupedlinear_kernel(tc, x, ln_gamma, ln_beta, W, b, out):
 
         def st_mx(g):
             acc = ps_o.tile([P, 4, P], F32, name="acc")
-            for d in range(DUMMY if g >= 0 else DUMMY_HEAD):
+            for d in range(DUMMY):
                 nc.tensor.matmul_mx(
                     out=acc[:].rearrange("p t r -> p (t r)"),
                     lhsT=zc[:, 0:P].bitcast(FP8X4),

@@ -20,20 +20,20 @@ FLOPS = 2 * G * P * K * N
 
 XB = 4
 NB = G // XB
-OUT_ON_SCALAR = (3, 7, 11, 15)
+OUT_ON_SCALAR = (11, 12, 13, 14)
 DUMMY = 0
-L_BS = 12
-L_SQ = 11
-L_RC = 11
-L_XH = 7
-L_XT = 6
-L_XE = 5
-L_RG = 4
-L_XQ = 4
-L_WT = 4
-L_WE = 3
-L_WQ = 2
-H0 = 3
+L_BS = 15
+L_SQ = 13
+L_RC = 12
+L_XH = 8
+L_XT = 7
+L_XE = 7
+L_RG = 6
+L_XQ = 6
+L_WT = 5
+L_WE = 5
+L_WQ = 3
+H0 = 4
 HS = 3
 
 
@@ -51,9 +51,9 @@ def tile_groupedlinear_kernel(tc, x, ln_gamma, ln_beta, W, b, out):
         keep = es.enter_context(tc.tile_pool(name="keep", bufs=1))
         wwork = es.enter_context(tc.tile_pool(name="wwork", bufs=6))
         owork = es.enter_context(tc.tile_pool(name="owork", bufs=6))
-        ps_w = es.enter_context(tc.psum_pool(name="ps_w", bufs=4))
-        ps_x = es.enter_context(tc.psum_pool(name="ps_x", bufs=2))
-        ps_o = es.enter_context(tc.psum_pool(name="ps_o", bufs=2))
+        ps_w = es.enter_context(tc.psum_pool(name="ps_w", bufs=2))
+        ps_x = es.enter_context(tc.psum_pool(name="ps_x", bufs=3))
+        ps_o = es.enter_context(tc.psum_pool(name="ps_o", bufs=3))
         es.enter_context(tc.manual_schedule())
 
         prm = const.tile([P, K], BF16, name="prm")
@@ -139,6 +139,8 @@ def tile_groupedlinear_kernel(tc, x, ln_gamma, ln_beta, W, b, out):
 
         def st_bs(j):
             nc.vector.bn_stats(out=stats[:, j, :], in_=xbs[j // XB][:, j % XB, :])
+
+        def st_ag(j):
             nc.vector.bn_aggr(out=mv[:, j, :], in_=stats[:, j, :])
 
         def st_sq(bi):
@@ -299,6 +301,9 @@ def tile_groupedlinear_kernel(tc, x, ln_gamma, ln_beta, W, b, out):
             j = group_at(s, L_BS)
             if j is not None:
                 st_bs(j)
+            j = group_at(s, L_BS - 1)
+            if j is not None:
+                st_ag(j)
             if s == first + H0 + 1:
                 params_out(p_t)
             bi = batch_at(s, L_RC)

@@ -24,7 +24,7 @@ OUT_ON_SCALAR = (11, 12, 13, 14)
 DUMMY = 0
 L_BS = 15
 L_SQ = 13
-L_RC = 12
+L_RC = 13
 L_XH = 8
 L_XT = 7
 L_XE = 7
@@ -33,8 +33,8 @@ L_XQ = 6
 L_WT = 5
 L_WE = 5
 L_WQ = 3
-H0 = 4
-HS = 3
+H0 = 6
+HS = 2
 
 
 def tile_groupedlinear_kernel(tc, x, ln_gamma, ln_beta, W, b, out):
@@ -77,9 +77,11 @@ def tile_groupedlinear_kernel(tc, x, ln_gamma, ln_beta, W, b, out):
 
         load_x(0, 0, 2)
         load_x(0, 2, 4)
+        load_x(1, 0, XB)
         load_w(0, 0, 2 * K)
         load_w(0, 2 * K, 4 * K)
-        for bi in range(1, NB):
+        load_w(1, 0, 4 * K)
+        for bi in range(2, NB):
             load_x(bi, 0, XB)
             load_w(bi, 0, 4 * K)
         for g in range(NB, G):
@@ -301,9 +303,10 @@ def tile_groupedlinear_kernel(tc, x, ln_gamma, ln_beta, W, b, out):
             j = group_at(s, L_BS)
             if j is not None:
                 st_bs(j)
-            j = group_at(s, L_BS - 1)
-            if j is not None:
-                st_ag(j)
+                if j % XB != 0:
+                    st_ag(j - 1)
+                if j % XB == XB - 1:
+                    st_ag(j)
             if s == first + H0 + 1:
                 params_out(p_t)
             bi = batch_at(s, L_RC)

@@ -20,7 +20,7 @@ FLOPS = 2 * G * P * K * N
 
 XB = 4
 NB = G // XB
-OUT_ON_SCALAR = (11, 12, 13, 14)
+OUT_ON_SCALAR = (10, 11, 12, 13, 14)
 DUMMY = 0
 L_BS = 15
 L_SQ = 13
@@ -227,6 +227,7 @@ def tile_groupedlinear_kernel(tc, x, ln_gamma, ln_beta, W, b, out):
 
         def st_mx(g):
             acc = ps_o.tile([P, 4, P], F32, name="acc")
+            acc2 = ps_o.tile([P, 4, P], F32, name="acc") if g == G - 1 else acc
             for d in range(DUMMY):
                 nc.tensor.matmul_mx(
                     out=acc[:].rearrange("p t r -> p (t r)"),
@@ -244,7 +245,7 @@ def tile_groupedlinear_kernel(tc, x, ln_gamma, ln_beta, W, b, out):
             i = g % XB
             for t in range(4):
                 nc.tensor.matmul_mx(
-                    out=acc[:, t, :],
+                    out=(acc if t < 2 else acc2)[:, t, :],
                     lhsT=wc[:, t * P:(t + 1) * P].bitcast(FP8X4),
                     lhsT_scale=ws[:, t * P:(t + 1) * P],
                     rhs=xc[:, i * P:(i + 1) * P].bitcast(FP8X4),
@@ -253,6 +254,24 @@ def tile_groupedlinear_kernel(tc, x, ln_gamma, ln_beta, W, b, out):
                     stop=True,
                 )
             acc_t[g] = acc
+            acc_t[g + G] = acc2
+
+        def st_oe_last_scalar(g):
+            acc = acc_t[g + G]
+            ot = owork.tile([P, 4, P], F32, name="ot")
+            for t in range(2, 4):
+                nc.scalar.activation(
+                    out=ot[:, t, :], in_=acc[:, t, :], func=ACT.Identity, bias=bias_t[:, g, t:t + 1], scale=1.0
+                )
+            nc.sync.dma_start(out=o_v[:, g, 2 * P:4 * P], in_=ot[:, 2:4, :].rearrange("p t r -> p (t r)"))
+
+        def st_oe_last_vector(g):
+            acc = acc_t[g]
+            ot = owork.tile([P, 4, P], F32, name="ot")
+            nc.vector.tensor_tensor(
+                out=ot[:, 0:2, :], in0=acc[:, 0:2, :], in1=bias_t[:, g, 0:2].unsqueeze(2).to_broadcast([P, 2, P]), op=ALU.add
+            )
+            nc.sync.dma_start(out=o_v[:, g, 0:2 * P], in_=ot[:, 0:2, :].rearrange("p t r -> p (t r)"))
 
         def st_oe(g):
             acc = acc_t[g]
@@ -300,6 +319,8 @@ def tile_groupedlinear_kernel(tc, x, ln_gamma, ln_beta, W, b, out):
                 st_xe(j)
             if s >= 0 and s in OUT_ON_SCALAR:
                 st_oe(s)
+            if s == G - 1:
+                st_oe_last_scalar(s)
             j = group_at(s, L_BS)
             if j is not None:
                 st_bs(j)
@@ -321,7 +342,9 @@ def tile_groupedlinear_kernel(tc, x, ln_gamma, ln_beta, W, b, out):
             bi = batch_at(s, L_RG)
             if bi is not None:
                 st_rg(bi)
-            if s >= 0 and s not in OUT_ON_SCALAR:
+            if s == G - 1:
+                st_oe_last_vector(s)
+            elif s >= 0 and s not in OUT_ON_SCALAR:
                 st_oe(s)
             bi = batch_at(s, L_XQ)
             if bi is not None:

@@ -20,7 +20,7 @@ FLOPS = 2 * G * P * K * N
 
 XB = 4
 NB = G // XB
-OUT_ON_SCALAR = (10, 11, 12, 13, 14)
+OUT_ON_SCALAR = (8, 10, 11, 12, 13, 14)
 DUMMY = 0
 L_BS = 15
 L_SQ = 13

@@ -20,7 +20,7 @@ FLOPS = 2 * G * P * K * N
 
 XB = 4
 NB = G // XB
-OUT_ON_SCALAR = (8, 10, 11, 12, 13, 14)
+OUT_ON_SCALAR = (8, 9, 10, 11, 12, 13, 14)
 DUMMY = 0
 L_BS = 15
 L_SQ = 13
@@ -324,9 +324,11 @@ def tile_groupedlinear_kernel(tc, x, ln_gamma, ln_beta, W, b, out):
             j = group_at(s, L_BS)
             if j is not None:
                 st_bs(j)
-                if j % XB != 0:
+                if j > XB:
                     st_ag(j - 1)
-                if j % XB == XB - 1:
+                elif j % XB != 0:
+                    st_ag(j - 1)
+                if j == XB - 1 or j == G - 1:
                     st_ag(j)
             if s == first + H0 + 1:
                 params_out(p_t)

@@ -47,12 +47,12 @@ def tile_groupedlinear_kernel(tc, x, ln_gamma, ln_beta, W, b, out):
         const = es.enter_context(tc.tile_pool(name="const", bufs=1))
         xin = es.enter_context(tc.tile_pool(name="xin", bufs=1))
         win = es.enter_context(tc.tile_pool(name="win", bufs=1))
-        xwork = es.enter_context(tc.tile_pool(name="xwork", bufs=2))
+        xwork = es.enter_context(tc.tile_pool(name="xwork", bufs=3))
         keep = es.enter_context(tc.tile_pool(name="keep", bufs=1))
-        wwork = es.enter_context(tc.tile_pool(name="wwork", bufs=6))
-        owork = es.enter_context(tc.tile_pool(name="owork", bufs=6))
-        ps_w = es.enter_context(tc.psum_pool(name="ps_w", bufs=2))
-        ps_x = es.enter_context(tc.psum_pool(name="ps_x", bufs=3))
+        wwork = es.enter_context(tc.tile_pool(name="wwork", bufs=8))
+        owork = es.enter_context(tc.tile_pool(name="owork", bufs=8))
+        ps_w = es.enter_context(tc.psum_pool(name="ps_w", bufs=3))
+        ps_x = es.enter_context(tc.psum_pool(name="ps_x", bufs=2))
         ps_o = es.enter_context(tc.psum_pool(name="ps_o", bufs=3))
         es.enter_context(tc.manual_schedule())
 
@@ -155,7 +155,7 @@ def tile_groupedlinear_kernel(tc, x, ln_gamma, ln_beta, W, b, out):
             nc.vector.tensor_scalar(out=negmu[:, sl, :], in0=mv[:, sl, 0:1], scalar1=-1.0, scalar2=None, op0=ALU.mult)
 
         def st_xh(j):
-            xh = xwork.tile([P, K], F32, name="xh", bufs=4)
+            xh = xwork.tile([P, K], F32, name="xh", bufs=6)
             nc.gpsimd.tensor_scalar(
                 out=xh[:].rearrange("p (u e q) -> p u e q", u=2, e=2),
                 in0=xbs[j // XB][:, j % XB, :].rearrange("p (u q e) -> p u e q", u=2, e=2),

@@ -80,10 +80,13 @@ def tile_groupedlinear_kernel(tc, x, ln_gamma, ln_beta, W, b, out):
         load_x(1, 0, XB)
         load_w(0, 0, 2 * K)
         load_w(0, 2 * K, 4 * K)
-        load_w(1, 0, 4 * K)
-        for bi in range(2, NB):
-            load_x(bi, 0, XB)
-            load_w(bi, 0, 4 * K)
+        load_w(1, 0, 2 * K)
+        load_w(1, 2 * K, 4 * K)
+        load_x(2, 0, XB)
+        for g in range(2, NB):
+            load_w(g, 0, 2 * K)
+            load_w(g, 2 * K, 4 * K)
+        load_x(3, 0, XB)
         for g in range(NB, G):
             load_w(g, 0, 4 * K)
 

@@ -75,18 +75,19 @@ def tile_groupedlinear_kernel(tc, x, ln_gamma, ln_beta, W, b, out):
         def load_w(g, lo, hi):
             nc.sync.dma_start(out=wraw[g][:, lo:hi], in_=w_v[:, g, lo:hi])
 
-        load_x(0, 0, 2)
-        load_x(0, 2, 4)
+        load_x(0, 0, 1)
+        load_x(0, 1, 2)
+        load_x(0, 2, XB)
         load_x(1, 0, XB)
         load_w(0, 0, 2 * K)
         load_w(0, 2 * K, 4 * K)
         load_w(1, 0, 2 * K)
         load_w(1, 2 * K, 4 * K)
-        load_x(2, 0, XB)
-        for g in range(2, NB):
-            load_w(g, 0, 2 * K)
-            load_w(g, 2 * K, 4 * K)
-        load_x(3, 0, XB)
+        for bi in range(2, NB):
+            load_x(bi, 0, 2)
+            load_w(bi, 0, 2 * K)
+            load_w(bi, 2 * K, 4 * K)
+            load_x(bi, 2, XB)
         for g in range(NB, G):
             load_w(g, 0, 4 * K)
 

@@ -59,8 +59,8 @@ def tile_groupedlinear_kernel(tc, x, ln_gamma, ln_beta, W, b, out):
         prm = const.tile([P, K], BF16, name="prm")
         nc.scalar.dma_start(out=prm[0:G, :], in_=ln_gamma)
         nc.scalar.dma_start(out=prm[G:2 * G, :], in_=ln_beta)
+        nc.vector.memset(prm[2 * G:4 * G, :], 0.0)
         nc.scalar.dma_start(out=prm[2 * G:3 * G, :], in_=b)
-        nc.scalar.dma_start(out=prm[3 * G:4 * G, :], in_=b)
 
         xbs = []
         wraw = []

from contextlib import ExitStack

import concourse.mybir as mybir
from concourse.masks import make_identity

F32 = mybir.dt.float32
BF16 = mybir.dt.bfloat16
U32 = mybir.dt.uint32
U8 = mybir.dt.uint8
FP8X4 = mybir.dt.float8_e4m3fn_x4
ALU = mybir.AluOpType
ACT = mybir.ActivationFunctionType

G = 16
P = 128
K = 512
N = 512
EPS = 1e-6
FLOPS = 2 * G * P * K * N

XB = 4
NB = G // XB
OUT_ON_SCALAR = (8, 9, 10, 11, 12, 13, 14)
DUMMY = 0
L_BS = 15
L_SQ = 13
L_RC = 13
L_XH = 8
L_XT = 7
L_XE = 7
L_RG = 6
L_XQ = 6
L_WT = 5
L_WE = 5
L_WQ = 3
H0 = 6
HS = 2


def tile_groupedlinear_kernel(tc, x, ln_gamma, ln_beta, W, b, out):
    nc = tc.nc
    x_v = x.rearrange("(g p j) b c d -> p g (j b c d)", g=G, p=P, j=4)
    w_v = W.rearrange("g (p t) k -> p g (t k)", t=4)
    o_v = out.rearrange("(g p t) b c d -> p g (t b c d)", g=G, p=P, t=4)

    with ExitStack() as es:
        const = es.enter_context(tc.tile_pool(name="const", bufs=1))
        xin = es.enter_context(tc.tile_pool(name="xin", bufs=1))
        win = es.enter_context(tc.tile_pool(name="win", bufs=1))
        xwork = es.enter_context(tc.tile_pool(name="xwork", bufs=3))
        keep = es.enter_context(tc.tile_pool(name="keep", bufs=1))
        wwork = es.enter_context(tc.tile_pool(name="wwork", bufs=8))
        owork = es.enter_context(tc.tile_pool(name="owork", bufs=8))
        ps_w = es.enter_context(tc.psum_pool(name="ps_w", bufs=3))
        ps_x = es.enter_context(tc.psum_pool(name="ps_x", bufs=2))
        ps_o = es.enter_context(tc.psum_pool(name="ps_o", bufs=3))
        es.enter_context(tc.manual_schedule())

        prm = const.tile([P, K], BF16, name="prm")
        nc.scalar.dma_start(out=prm[0:G, :], in_=ln_gamma)
        nc.scalar.dma_start(out=prm[G:2 * G, :], in_=ln_beta)
        nc.vector.memset(prm[2 * G:4 * G, :], 0.0)
        nc.scalar.dma_start(out=prm[2 * G:3 * G, :], in_=b)

        xbs = []
        wraw = []
        for bi in range(NB):
            xbs.append(xin.tile([P, XB, K], BF16, name="xb%d" % bi))
        for g in range(G):
            wraw.append(win.tile([P, 4 * K], BF16, name="wr%d" % g))

        def load_x(bi, lo, hi):
            nc.sync.dma_start(out=xbs[bi][:, lo:hi, :], in_=x_v[:, XB * bi + lo:XB * bi + hi, :])

        def load_w(g, lo, hi):
            nc.sync.dma_start(out=wraw[g][:, lo:hi], in_=w_v[:, g, lo:hi])

        load_x(0, 0, 1)
        load_x(0, 1, 2)
        load_x(0, 2, XB)
        load_x(1, 0, XB)
        load_w(0, 0, 2 * K)
        load_w(0, 2 * K, 4 * K)
        load_w(1, 0, 2 * K)
        load_w(1, 2 * K, 4 * K)
        for bi in range(2, NB):
            load_x(bi, 0, 2)
            load_w(bi, 0, 2 * K)
            load_w(bi, 2 * K, 4 * K)
            load_x(bi, 2, XB)
        for g in range(NB, G):
            load_w(g, 0, 4 * K)

        eps_t = const.tile([P, 1], F32, name="eps_t")
        nc.vector.memset(eps_t[:], EPS)
        warm = const.tile([P, 1], F32, name="warm")
        nc.scalar.activation(out=warm[:], in_=eps_t[:], func=ACT.Sqrt)
        nc.vector.memset(prm[4 * G:P, :], 0.0)
        if DUMMY:
            zb = const.tile([P, 4 * N], BF16, name="zb", align_bytes=64)
            zc = const.tile([P, N], U32, name="zc", align_bytes=64)
            zs = const.tile([P, N], U8, name="zs", align_bytes=64)
            nc.vector.memset(zb[:], 0.0)
            nc.vector.quantize_mx(out=zc[:].bitcast(FP8X4), scales=zs[:], in_=zb[:])
        ident = const.tile([P, P], F32, name="ident")
        make_identity(nc, ident[:])

        gb_t = const.tile([P, 2 * G, 4], F32, name="gb_t")
        bias_t = const.tile([P, G, 4], F32, name="bias_t")
        stats = const.tile([P, G, 6], F32, name="stats")
        mv = const.tile([P, G, 2], F32, name="mv")
        std = const.tile([P, G, 1], F32, name="std")
        rstd = const.tile([P, G, 1], F32, name="rstd")
        negmu = const.tile([P, G, 1], F32, name="negmu")

        def params_pe():
            prm_w = prm[:].bitcast(F32)
            p_t = ps_x.tile([P, 4, P], F32, name="xT")
            nc.tensor.transpose(p_t[:, 0, :], prm_w[:, 0:P], ident[:])
            nc.tensor.transpose(p_t[:, 1, :], prm_w[:, P:2 * P], ident[:])
            nc.tensor.transpose(p_t[:, 2, :], prm_w[:, 0:2 * P:2], ident[:])
            nc.tensor.transpose(p_t[:, 3, :], prm_w[:, 1:2 * P:2], ident[:])
            return p_t

        def params_out(p_t):
            p_b = p_t[:].rearrange("q j r -> q (j r)").bitcast(BF16).rearrange("q (j r e) -> q j r e", j=4, e=2)
            nc.vector.tensor_copy(
                out=gb_t[:].rearrange("q r (u e) -> q r u e", u=2),
                in_=p_b[:, 0:2, 0:2 * G, :].rearrange("q u r e -> q r u e"),
            )
            nc.vector.tensor_copy(
                out=bias_t[:].rearrange("q r (u e) -> q r u e", u=2),
                in_=p_b[:, 2:4, 2 * G:3 * G, :].rearrange("q u r e -> q r u e"),
            )

        xh_t = {}
        xt_t = {}
        xp_t = {}
        xg_t = {}
        xc_t = {}
        wt_t = {}
        wg_t = {}
        wc_t = {}
        acc_t = {}

        def st_bs(j):
            nc.vector.bn_stats(out=stats[:, j, :], in_=xbs[j // XB][:, j % XB, :])

        def st_ag(j):
            nc.vector.bn_aggr(out=mv[:, j, :], in_=stats[:, j, :])

        def st_sq(bi):
            sl = slice(XB * bi, XB * (bi + 1))
            nc.scalar.activation(out=std[:, sl, :], in_=mv[:, sl, 1:2], func=ACT.Sqrt, bias=eps_t[:, 0:1], scale=1.0)

        def st_rc(bi):
            sl = slice(XB * bi, XB * (bi + 1))
            nc.vector.reciprocal(out=rstd[:, sl, :], in_=std[:, sl, :])
            nc.vector.tensor_scalar(out=negmu[:, sl, :], in0=mv[:, sl, 0:1], scalar1=-1.0, scalar2=None, op0=ALU.mult)

        def st_xh(j):
            xh = xwork.tile([P, K], F32, name="xh", bufs=6)
            nc.gpsimd.tensor_scalar(
                out=xh[:].rearrange("p (u e q) -> p u e q", u=2, e=2),
                in0=xbs[j // XB][:, j % XB, :].rearrange("p (u q e) -> p u e q", u=2, e=2),
                scalar1=negmu[:, j, :],
                scalar2=rstd[:, j, :],
                op0=ALU.add,
                op1=ALU.mult,
            )
            xh_t[j] = xh

        def st_xt(j):
            x_t = ps_x.tile([P, 4, P], F32, name="xT")
            for t in range(4):
                nc.tensor.transpose(x_t[:, t, :], xh_t[j][:, t * P:(t + 1) * P], ident[:])
            xt_t[j] = x_t

        def st_xe(j):
            bi = j // XB
            if j % XB == 0:
                xp_t[bi] = xwork.tile([P, 4, XB, P], BF16, name="xp")
            for t in range(4):
                nc.scalar.activation(
                    out=xp_t[bi][:, t, j % XB, :],
                    in_=xt_t[j][:, t, :],
                    func=ACT.Identity,
                    scale=gb_t[:, j, t:t + 1],
                    bias=gb_t[:, G + j, t:t + 1],
                )

        def st_rg(bi):
            xg = xwork.tile([P, XB * P * 4], BF16, name="xg", align_bytes=64)
            nc.vector.tensor_copy(
                out=xg[:].rearrange("p (c i t) -> p c t i", i=4, t=4),
                in_=xp_t[bi][:].rearrange("p t g r -> p t (g r)").rearrange("p t (c i) -> p c t i", i=4),
            )
            xg_t[bi] = xg

        def st_xq(bi):
            xc = keep.tile([P, XB * P], U32, name="xc%d" % bi, align_bytes=64)
            xs = keep.tile([P, XB * P], U8, name="xs%d" % bi, align_bytes=64)
            nc.vector.quantize_mx(out=xc[:].bitcast(FP8X4), scales=xs[:], in_=xg_t[bi][:])
            xc_t[bi] = (xc, xs)

        def st_wt(g):
            wf = wraw[g][:].bitcast(F32)
            for h in range(2):
                w_t = ps_w.tile([P, 2, 2, P], F32, name="wT")
                for tt in range(2):
                    for u in range(2):
                        c0 = (2 * h + tt) * 256 + u * P
                        nc.tensor.transpose(w_t[:, tt, u, :], wf[:, c0:c0 + P], ident[:])
                wt_t[(g, h)] = w_t

        def st_we(g):
            wg = wwork.tile([P, 4 * N], BF16, name="wg", align_bytes=64)
            wgf = wg[:].bitcast(F32)
            for h in range(2):
                nc.scalar.copy(
                    out=wgf[:, h * 512:(h + 1) * 512].rearrange("q (tt p u) -> q tt p u", tt=2, u=2),
                    in_=wt_t[(g, h)][:].rearrange("q tt u p -> q tt p u"),
                )
            wg_t[g] = wg

        def st_wq(g):
            wc = keep.tile([P, N], U32, name="wc%d" % g, align_bytes=64)
            ws = keep.tile([P, N], U8, name="ws%d" % g, align_bytes=64)
            nc.vector.quantize_mx(out=wc[:].bitcast(FP8X4), scales=ws[:], in_=wg_t[g][:])
            wc_t[g] = (wc, ws)

        def st_mx(g):
            acc = ps_o.tile([P, 4, P], F32, name="acc")
            acc2 = ps_o.tile([P, 4, P], F32, name="acc") if g == G - 1 else acc
            for d in range(DUMMY):
                nc.tensor.matmul_mx(
                    out=acc[:].rearrange("p t r -> p (t r)"),
                    lhsT=zc[:, 0:P].bitcast(FP8X4),
                    lhsT_scale=zs[:, 0:P],
                    rhs=zc[:].bitcast(FP8X4),
                    rhs_scale=zs[:],
                    start=True,
                    stop=True,
                )
            if g < 0:
                return
            wc, ws = wc_t[g]
            xc, xs = xc_t[g // XB]
            i = g % XB
            for t in range(4):
                nc.tensor.matmul_mx(
                    out=(acc if t < 2 else acc2)[:, t, :],
                    lhsT=wc[:, t * P:(t + 1) * P].bitcast(FP8X4),
                    lhsT_scale=ws[:, t * P:(t + 1) * P],
                    rhs=xc[:, i * P:(i + 1) * P].bitcast(FP8X4),
                    rhs_scale=xs[:, i * P:(i + 1) * P],
                    start=True,
                    stop=True,
                )
            acc_t[g] = acc
            acc_t[g + G] = acc2

        def st_oe_last_scalar(g):
            acc = acc_t[g + G]
            ot = owork.tile([P, 4, P], F32, name="ot")
            for t in range(2, 4):
                nc.scalar.activation(
                    out=ot[:, t, :], in_=acc[:, t, :], func=ACT.Identity, bias=bias_t[:, g, t:t + 1], scale=1.0
                )
            nc.sync.dma_start(out=o_v[:, g, 2 * P:4 * P], in_=ot[:, 2:4, :].rearrange("p t r -> p (t r)"))

        def st_oe_last_vector(g):
            acc = acc_t[g]
            ot = owork.tile([P, 4, P], F32, name="ot")
            nc.vector.tensor_tensor(
                out=ot[:, 0:2, :], in0=acc[:, 0:2, :], in1=bias_t[:, g, 0:2].unsqueeze(2).to_broadcast([P, 2, P]), op=ALU.add
            )
            nc.sync.dma_start(out=o_v[:, g, 0:2 * P], in_=ot[:, 0:2, :].rearrange("p t r -> p (t r)"))

        def st_oe(g):
            acc = acc_t[g]
            ot = owork.tile([P, 4, P], F32, name="ot")
            if g in OUT_ON_SCALAR:
                for t in range(4):
                    nc.scalar.activation(
                        out=ot[:, t, :], in_=acc[:, t, :], func=ACT.Identity, bias=bias_t[:, g, t:t + 1], scale=1.0
                    )
            else:
                nc.vector.tensor_tensor(
                    out=ot[:], in0=acc[:], in1=bias_t[:, g, :].unsqueeze(2).to_broadcast([P, 4, P]), op=ALU.add
                )
            nc.sync.dma_start(out=o_v[:, g, :], in_=ot[:].rearrange("p t r -> p (t r)"))

        def group_at(s, lead):
            j = s + lead
            return j if 0 <= j < G else None

        def batch_at(s, lead):
            j = s + lead
            return j // XB if (0 <= j < G and j % XB == XB - 1) else None

        def w_groups_at(s, lead):
            return [g for g in range(G) if min(g - lead, H0 - L_BS + HS * g) == s]

        first = -L_BS
        for s in range(first, G):
            for g in w_groups_at(s, L_WT):
                st_wt(g)
            if s == first + H0 + 1:
                p_t = params_pe()
            j = group_at(s, L_XT)
            if j is not None:
                st_xt(j)
            if s >= 0 or DUMMY:
                st_mx(s)
            for g in w_groups_at(s, L_WE):
                st_we(g)
            bi = batch_at(s, L_SQ)
            if bi is not None:
                st_sq(bi)
            j = group_at(s, L_XE)
            if j is not None:
                st_xe(j)
            if s >= 0 and s in OUT_ON_SCALAR:
                st_oe(s)
            if s == G - 1:
                st_oe_last_scalar(s)
            j = group_at(s, L_BS)
            if j is not None:
                st_bs(j)
                if j > XB:
                    st_ag(j - 1)
                elif j % XB != 0:
                    st_ag(j - 1)
                if j == XB - 1 or j == G - 1:
                    st_ag(j)
            if s == first + H0 + 1:
                params_out(p_t)
            bi = batch_at(s, L_RC)
            if bi is not None:
                st_rc(bi)
            j = group_at(s, L_XH)
            if j is not None:
                st_xh(j)
            j = group_at(s, L_WQ)
            if j is not None:
                st_wq(j)
            bi = batch_at(s, L_RG)
            if bi is not None:
                st_rg(bi)
            if s == G - 1:
                st_oe_last_vector(s)
            elif s >= 0 and s not in OUT_ON_SCALAR:
                st_oe(s)
            bi = batch_at(s, L_XQ)
            if bi is not None:
                st_xq(bi)
